import numpy as np
import ml_dtypes

BF16 = ml_dtypes.bfloat16


def bf(x):
    return np.asarray(x, np.float32).astype(BF16)


def f32(x):
    return np.asarray(x, np.float32)


def f64(x):
    return np.asarray(x).astype(np.float64)


def striped(idx):
    return np.tile(idx.reshape(-1, 16).T, (8, 1))


C, C2, S, M, B, N = 128, 256, 512, 4, 512, 2048
STAB = 10.0
AGES = np.arange(M - 1, -1, -1).astype(np.float64)
WGT = np.exp(-AGES * (AGES + 1.0) / (2.0 * STAB))


def setup_inputs():
    return {"table": f32(np.random.standard_normal((C, S))), "q": bf(np.random.standard_normal((C, B))), "w1": bf(np.random.standard_normal((C2, C)) / np.sqrt(C2)), "b1": f32(0.1 * np.random.standard_normal((C, 1))), "w2": bf(np.random.standard_normal((C, S)) / np.sqrt(C)), "b2": f32(0.1 * np.random.standard_normal((S, 1))), "offs": striped(np.concatenate([np.random.permutation(S) for _ in range(M)]))}


def reference(table, q, w1, b1, w2, b2, offs):
    idx = offs[:16].T.reshape(-1)
    picked = f64(table)[:, idx].reshape(C, M, B)
    mem = (picked * WGT[None, :, None]).sum(axis=1) / M
    h0 = np.concatenate([f64(q), mem], axis=0)
    hid = np.maximum(f64(w1).T @ h0 + f64(b1), 0.0)
    return f64(w2).T @ hid + f64(b2)

@@ -1,0 +1,105 @@
+import math
+from contextlib import ExitStack
+
+import concourse.mybir as mybir
+
+F32, BF16, U16 = mybir.dt.float32, mybir.dt.bfloat16, mybir.dt.uint16
+MULT, ADD = mybir.AluOpType.mult, mybir.AluOpType.add
+RELU = mybir.ActivationFunctionType.Relu
+IDENTITY = mybir.ActivationFunctionType.Identity
+
+P = 128
+WORDS = 512
+SAMPLES = 512
+SLOTS = 4
+VBLOCKS = 4
+WGT = [math.exp(-age * (age + 1) / 20.0) for age in (3, 2, 1, 0)]
+
+WIDTHS = (192, 192, 128)
+assert sum(WIDTHS) == SAMPLES
+
+FLOPS = 2 * 256 * P * SAMPLES + 2 * P * 512 * SAMPLES
+
+
+def tile_ebbinghausmodel_kernel(tc, table, q, w1, b1, w2, b2, offs, out):
+    nc = tc.nc
+    with ExitStack() as ctx:
+        held = ctx.enter_context(tc.tile_pool(name="held", bufs=1))
+        work = ctx.enter_context(tc.tile_pool(name="work", bufs=len(WIDTHS)))
+        sums = ctx.enter_context(tc.tile_pool(name="sums", bufs=1))
+        psum_hid = ctx.enter_context(tc.psum_pool(name="psum_hid", bufs=2))
+        psum_out = ctx.enter_context(tc.psum_pool(name="psum_out", bufs=6))
+
+        table_sb = held.tile([P, WORDS], F32, name="table_sb")
+        nc.sync.dma_start(table_sb[:], table)
+        offsets = held.tile([P, SLOTS * SAMPLES // 16], U16, name="offsets")
+        nc.sync.dma_start(offsets[:], offs)
+        w1_sb = held.tile([P, 2, P], BF16, name="w1_sb")
+        nc.sync.dma_start(w1_sb[:], w1.rearrange("(half k) d -> k half d", k=P))
+        q_sb = held.tile([P, SAMPLES], BF16, name="q_sb")
+        nc.sync.dma_start(q_sb[:], q)
+        b1_sb = held.tile([P, 1], F32, name="b1_sb")
+        nc.sync.dma_start(b1_sb[:], b1)
+        w2_sb = held.tile([P, VBLOCKS * P], BF16, name="w2_sb")
+        nc.sync.dma_start(w2_sb[:], w2)
+        b2_sb = held.tile([P, VBLOCKS], F32, name="b2_sb")
+        with nc.allow_non_contiguous_dma(reason="512 floats, one to a partition and block"):
+            nc.sync.dma_start(b2_sb[:], b2.rearrange("(v p) one -> p (v one)", p=P))
+        out_blocks = out.rearrange("(v p) n -> p v n", p=P)
+
+        decay_older = held.tile([P, max(WIDTHS)], F32, name="decay_older")
+        nc.vector.memset(decay_older[:], WGT[0] / WGT[1])
+        decay_newer = held.tile([P, max(WIDTHS)], F32, name="decay_newer")
+        nc.vector.memset(decay_newer[:], WGT[2])
+        w1_mem = held.tile([P, P], BF16, name="w1_mem")
+        nc.scalar.mul(w1_mem[:], w1_sb[:, 1, :], 1.0 / SLOTS)
+
+        def add_bias_and_store(first, width, out_sb, out_ps, pair):
+            for v in pair:
+                if first + width == SAMPLES and v % 2 == 0:
+                    nc.vector.tensor_scalar_add(out_sb[:, v, :], out_ps[v][:], b2_sb[:, v : v + 1])
+                else:
+                    nc.scalar.activation(out_sb[:, v, :], out_ps[v][:], IDENTITY, bias=b2_sb[:, v : v + 1])
+            nc.sync.dma_start(
+                out_blocks[:, pair[0] : pair[1] + 1, first : first + width], out_sb[:, pair[0] : pair[1] + 1, :]
+            )
+
+        first = 0
+        for width in WIDTHS:
+            picked = []
+            for t in range(SLOTS):
+                column = (t * SAMPLES + first) // 16
+                picked.append(table_sb[:].indirect(offsets[:, column : column + width // 16]))
+
+            hid_ps = psum_hid.tile([P, width], F32, name="hid_ps")
+            nc.tensor.matmul(
+                hid_ps[:], w1_sb[:, 0, :], q_sb[:, first : first + width], start=True, stop=False
+            )
+
+            faded0 = sums.tile([P, width], F32, name="faded0")
+            nc.vector.tensor_tensor(faded0[:], picked[0], decay_older[:, :width], MULT)
+            faded2 = sums.tile([P, width], F32, name="faded2")
+            nc.vector.tensor_tensor(faded2[:], picked[2], decay_newer[:, :width], MULT)
+            older = sums.tile([P, width], F32, name="older")
+            nc.vector.tensor_tensor(older[:], picked[1], faded0[:], ADD)
+            newer = sums.tile([P, width], F32, name="newer")
+            nc.vector.tensor_tensor(newer[:], picked[3], faded2[:], ADD)
+            mem4 = work.tile([P, width], BF16, name="mem4")
+            nc.vector.scalar_tensor_tensor(mem4[:], older[:], WGT[1], newer[:], op0=MULT, op1=ADD)
+
+            nc.tensor.matmul(hid_ps[:], w1_mem[:], mem4[:], start=False, stop=True)
+            hid = work.tile([P, width], BF16, name="hid")
+            nc.scalar.activation(hid[:], hid_ps[:], RELU, bias=b1_sb[:, 0:1])
+
+            if first > 0:
+                add_bias_and_store(before[0], before[1], out_sb, out_ps, (2, 3))
+
+            out_sb = work.tile([P, VBLOCKS, width], F32, name="out_sb")
+            out_ps = []
+            for v in range(VBLOCKS):
+                out_ps.append(psum_out.tile([P, width], F32, name="out_ps"))
+                nc.tensor.matmul(out_ps[v][:], w2_sb[:, v * P : (v + 1) * P], hid[:], start=True, stop=True)
+            add_bias_and_store(first, width, out_sb, out_ps, (0, 1))
+            before = (first, width)
+            first += width
+        add_bias_and_store(before[0], before[1], out_sb, out_ps, (2, 3))

@@ -27,8 +27,8 @@ def tile_ebbinghausmodel_kernel(tc, table, q, w1, b1, w2, b2, offs, out):
         held = ctx.enter_context(tc.tile_pool(name="held", bufs=1))
         work = ctx.enter_context(tc.tile_pool(name="work", bufs=len(WIDTHS)))
         sums = ctx.enter_context(tc.tile_pool(name="sums", bufs=1))
-        psum_hid = ctx.enter_context(tc.psum_pool(name="psum_hid", bufs=2))
-        psum_out = ctx.enter_context(tc.psum_pool(name="psum_out", bufs=6))
+        psum_hid = ctx.enter_context(tc.psum_pool(name="psum_hid", bufs=1))
+        psum_out = ctx.enter_context(tc.psum_pool(name="psum_out", bufs=7))
 
         table_sb = held.tile([P, WORDS], F32, name="table_sb")
         nc.sync.dma_start(table_sb[:], table)

@@ -4,7 +4,7 @@ from contextlib import ExitStack
 import concourse.mybir as mybir
 
 F32, BF16, U16 = mybir.dt.float32, mybir.dt.bfloat16, mybir.dt.uint16
-MULT, ADD = mybir.AluOpType.mult, mybir.AluOpType.add
+MULT, ADD, MAX = mybir.AluOpType.mult, mybir.AluOpType.add, mybir.AluOpType.max
 RELU = mybir.ActivationFunctionType.Relu
 IDENTITY = mybir.ActivationFunctionType.Identity
 
@@ -56,7 +56,7 @@ def tile_ebbinghausmodel_kernel(tc, table, q, w1, b1, w2, b2, offs, out):
 
         def add_bias_and_store(first, width, out_sb, out_ps, pair):
             for v in pair:
-                if first + width == SAMPLES and v % 2 == 0:
+                if first + width + WIDTHS[-1] >= SAMPLES and v % 2 == 0:
                     nc.vector.tensor_scalar_add(out_sb[:, v, :], out_ps[v][:], b2_sb[:, v : v + 1])
                 else:
                     nc.scalar.activation(out_sb[:, v, :], out_ps[v][:], IDENTITY, bias=b2_sb[:, v : v + 1])
@@ -89,10 +89,10 @@ def tile_ebbinghausmodel_kernel(tc, table, q, w1, b1, w2, b2, offs, out):
 
             nc.tensor.matmul(hid_ps[:], w1_mem[:], mem4[:], start=False, stop=True)
             hid = work.tile([P, width], BF16, name="hid")
-            nc.scalar.activation(hid[:], hid_ps[:], RELU, bias=b1_sb[:, 0:1])
-
-            if first > 0:
-                add_bias_and_store(before[0], before[1], out_sb, out_ps, (2, 3))
+            if first + width < SAMPLES:
+                nc.scalar.activation(hid[:], hid_ps[:], RELU, bias=b1_sb[:, 0:1])
+            else:
+                nc.vector.tensor_scalar(hid[:], hid_ps[:], b1_sb[:, 0:1], 0.0, op0=ADD, op1=MAX)
 
             out_sb = work.tile([P, VBLOCKS, width], F32, name="out_sb")
             out_ps = []
@@ -100,6 +100,5 @@ def tile_ebbinghausmodel_kernel(tc, table, q, w1, b1, w2, b2, offs, out):
                 out_ps.append(psum_out.tile([P, width], F32, name="out_ps"))
                 nc.tensor.matmul(out_ps[v][:], w2_sb[:, v * P : (v + 1) * P], hid[:], start=True, stop=True)
             add_bias_and_store(first, width, out_sb, out_ps, (0, 1))
-            before = (first, width)
+            add_bias_and_store(first, width, out_sb, out_ps, (2, 3))
             first += width
-        add_bias_and_store(before[0], before[1], out_sb, out_ps, (2, 3))

@@ -15,7 +15,7 @@ SLOTS = 4
 VBLOCKS = 4
 WGT = [math.exp(-age * (age + 1) / 20.0) for age in (3, 2, 1, 0)]
 
-WIDTHS = (192, 192, 128)
+WIDTHS = (224, 160, 128)
 assert sum(WIDTHS) == SAMPLES
 
 FLOPS = 2 * 256 * P * SAMPLES + 2 * P * 512 * SAMPLES
@@ -54,9 +54,13 @@ def tile_ebbinghausmodel_kernel(tc, table, q, w1, b1, w2, b2, offs, out):
         w1_mem = held.tile([P, P], BF16, name="w1_mem")
         nc.scalar.mul(w1_mem[:], w1_sb[:, 1, :], 1.0 / SLOTS)
 
-        def add_bias_and_store(first, width, out_sb, out_ps, pair):
+        def second_layer(first, width, hid, out_sb, pair):
+            out_ps = {}
             for v in pair:
-                if first + width + WIDTHS[-1] >= SAMPLES and v % 2 == 0:
+                out_ps[v] = psum_out.tile([P, width], F32, name="out_ps")
+                nc.tensor.matmul(out_ps[v][:], w2_sb[:, v * P : (v + 1) * P], hid[:], start=True, stop=True)
+            for v in pair:
+                if first + width + WIDTHS[-1] >= SAMPLES and v % 2 == 1:
                     nc.vector.tensor_scalar_add(out_sb[:, v, :], out_ps[v][:], b2_sb[:, v : v + 1])
                 else:
                     nc.scalar.activation(out_sb[:, v, :], out_ps[v][:], IDENTITY, bias=b2_sb[:, v : v + 1])
@@ -94,11 +98,10 @@ def tile_ebbinghausmodel_kernel(tc, table, q, w1, b1, w2, b2, offs, out):
             else:
                 nc.vector.tensor_scalar(hid[:], hid_ps[:], b1_sb[:, 0:1], 0.0, op0=ADD, op1=MAX)
 
+            if first > 0:
+                second_layer(*before, (2, 3))
             out_sb = work.tile([P, VBLOCKS, width], F32, name="out_sb")
-            out_ps = []
-            for v in range(VBLOCKS):
-                out_ps.append(psum_out.tile([P, width], F32, name="out_ps"))
-                nc.tensor.matmul(out_ps[v][:], w2_sb[:, v * P : (v + 1) * P], hid[:], start=True, stop=True)
-            add_bias_and_store(first, width, out_sb, out_ps, (0, 1))
-            add_bias_and_store(first, width, out_sb, out_ps, (2, 3))
+            second_layer(first, width, hid, out_sb, (0, 1))
+            before = (first, width, hid, out_sb)
             first += width
+        second_layer(*before, (2, 3))

@@ -71,7 +71,7 @@ def tile_ebbinghausmodel_kernel(tc, table, q, w1, b1, w2, b2, offs, out):
         first = 0
         for width in WIDTHS:
             picked = []
-            for t in range(SLOTS):
+            for t in range(SLOTS - 1):
                 column = (t * SAMPLES + first) // 16
                 picked.append(table_sb[:].indirect(offsets[:, column : column + width // 16]))
 
@@ -86,12 +86,22 @@ def tile_ebbinghausmodel_kernel(tc, table, q, w1, b1, w2, b2, offs, out):
             nc.vector.tensor_tensor(faded2[:], picked[2], decay_newer[:, :width], MULT)
             older = sums.tile([P, width], F32, name="older")
             nc.vector.tensor_tensor(older[:], picked[1], faded0[:], ADD)
+            if first + width < SAMPLES:
+                parts = [slice(0, width)]
+            else:
+                parts = [slice(0, width // 2), slice(width // 2, width)]
             newer = sums.tile([P, width], F32, name="newer")
-            nc.vector.tensor_tensor(newer[:], picked[3], faded2[:], ADD)
+            for part in parts:
+                column = (3 * SAMPLES + first + part.start) // 16
+                looked_up = table_sb[:].indirect(offsets[:, column : column + (part.stop - part.start) // 16])
+                nc.vector.tensor_tensor(newer[:, part], looked_up, faded2[:, part], ADD)
             mem4 = work.tile([P, width], BF16, name="mem4")
-            nc.vector.scalar_tensor_tensor(mem4[:], older[:], WGT[1], newer[:], op0=MULT, op1=ADD)
-
-            nc.tensor.matmul(hid_ps[:], w1_mem[:], mem4[:], start=False, stop=True)
+            for part in parts:
+                nc.vector.scalar_tensor_tensor(
+                    mem4[:, part], older[:, part], WGT[1], newer[:, part], op0=MULT, op1=ADD
+                )
+            for part in parts:
+                nc.tensor.matmul(hid_ps[:, part], w1_mem[:], mem4[:, part], start=False, stop=part.stop == width)
             hid = work.tile([P, width], BF16, name="hid")
             if first + width < SAMPLES:
                 nc.scalar.activation(hid[:], hid_ps[:], RELU, bias=b1_sb[:, 0:1])

import math
from contextlib import ExitStack

import concourse.mybir as mybir

F32, BF16, U16 = mybir.dt.float32, mybir.dt.bfloat16, mybir.dt.uint16
MULT, ADD, MAX = mybir.AluOpType.mult, mybir.AluOpType.add, mybir.AluOpType.max
RELU = mybir.ActivationFunctionType.Relu
IDENTITY = mybir.ActivationFunctionType.Identity

P = 128
WORDS = 512
SAMPLES = 512
SLOTS = 4
VBLOCKS = 4
WGT = [math.exp(-age * (age + 1) / 20.0) for age in (3, 2, 1, 0)]

WIDTHS = (224, 160, 128)
assert sum(WIDTHS) == SAMPLES

FLOPS = 2 * 256 * P * SAMPLES + 2 * P * 512 * SAMPLES


def tile_ebbinghausmodel_kernel(tc, table, q, w1, b1, w2, b2, offs, out):
    nc = tc.nc
    with ExitStack() as ctx:
        held = ctx.enter_context(tc.tile_pool(name="held", bufs=1))
        work = ctx.enter_context(tc.tile_pool(name="work", bufs=len(WIDTHS)))
        sums = ctx.enter_context(tc.tile_pool(name="sums", bufs=1))
        psum_hid = ctx.enter_context(tc.psum_pool(name="psum_hid", bufs=1))
        psum_out = ctx.enter_context(tc.psum_pool(name="psum_out", bufs=7))

        table_sb = held.tile([P, WORDS], F32, name="table_sb")
        nc.sync.dma_start(table_sb[:], table)
        offsets = held.tile([P, SLOTS * SAMPLES // 16], U16, name="offsets")
        nc.sync.dma_start(offsets[:], offs)
        w1_sb = held.tile([P, 2, P], BF16, name="w1_sb")
        nc.sync.dma_start(w1_sb[:], w1.rearrange("(half k) d -> k half d", k=P))
        q_sb = held.tile([P, SAMPLES], BF16, name="q_sb")
        nc.sync.dma_start(q_sb[:], q)
        b1_sb = held.tile([P, 1], F32, name="b1_sb")
        nc.sync.dma_start(b1_sb[:], b1)
        w2_sb = held.tile([P, VBLOCKS * P], BF16, name="w2_sb")
        nc.sync.dma_start(w2_sb[:], w2)
        b2_sb = held.tile([P, VBLOCKS], F32, name="b2_sb")
        with nc.allow_non_contiguous_dma(reason="512 floats, one to a partition and block"):
            nc.sync.dma_start(b2_sb[:], b2.rearrange("(v p) one -> p (v one)", p=P))
        out_blocks = out.rearrange("(v p) n -> p v n", p=P)

        decay_older = held.tile([P, max(WIDTHS)], F32, name="decay_older")
        nc.vector.memset(decay_older[:], WGT[0] / WGT[1])
        decay_newer = held.tile([P, max(WIDTHS)], F32, name="decay_newer")
        nc.vector.memset(decay_newer[:], WGT[2])
        w1_mem = held.tile([P, P], BF16, name="w1_mem")
        nc.scalar.mul(w1_mem[:], w1_sb[:, 1, :], 1.0 / SLOTS)

        def second_layer(first, width, hid, out_sb, pair):
            out_ps = {}
            for v in pair:
                out_ps[v] = psum_out.tile([P, width], F32, name="out_ps")
                nc.tensor.matmul(out_ps[v][:], w2_sb[:, v * P : (v + 1) * P], hid[:], start=True, stop=True)
            for v in pair:
                if first + width + WIDTHS[-1] >= SAMPLES and v % 2 == 1:
                    nc.vector.tensor_scalar_add(out_sb[:, v, :], out_ps[v][:], b2_sb[:, v : v + 1])
                else:
                    nc.scalar.activation(out_sb[:, v, :], out_ps[v][:], IDENTITY, bias=b2_sb[:, v : v + 1])
            nc.sync.dma_start(
                out_blocks[:, pair[0] : pair[1] + 1, first : first + width], out_sb[:, pair[0] : pair[1] + 1, :]
            )

        first = 0
        for width in WIDTHS:
            picked = []
            for t in range(SLOTS - 1):
                column = (t * SAMPLES + first) // 16
                picked.append(table_sb[:].indirect(offsets[:, column : column + width // 16]))

            hid_ps = psum_hid.tile([P, width], F32, name="hid_ps")
            nc.tensor.matmul(
                hid_ps[:], w1_sb[:, 0, :], q_sb[:, first : first + width], start=True, stop=False
            )

            faded0 = sums.tile([P, width], F32, name="faded0")
            nc.vector.tensor_tensor(faded0[:], picked[0], decay_older[:, :width], MULT)
            faded2 = sums.tile([P, width], F32, name="faded2")
            nc.vector.tensor_tensor(faded2[:], picked[2], decay_newer[:, :width], MULT)
            older = sums.tile([P, width], F32, name="older")
            nc.vector.tensor_tensor(older[:], picked[1], faded0[:], ADD)
            if first + width < SAMPLES:
                parts = [slice(0, width)]
            else:
                parts = [slice(0, width // 2), slice(width // 2, width)]
            newer = sums.tile([P, width], F32, name="newer")
            for part in parts:
                column = (3 * SAMPLES + first + part.start) // 16
                looked_up = table_sb[:].indirect(offsets[:, column : column + (part.stop - part.start) // 16])
                nc.vector.tensor_tensor(newer[:, part], looked_up, faded2[:, part], ADD)
            mem4 = work.tile([P, width], BF16, name="mem4")
            for part in parts:
                nc.vector.scalar_tensor_tensor(
                    mem4[:, part], older[:, part], WGT[1], newer[:, part], op0=MULT, op1=ADD
                )
            for part in parts:
                nc.tensor.matmul(hid_ps[:, part], w1_mem[:], mem4[:, part], start=False, stop=part.stop == width)
            hid = work.tile([P, width], BF16, name="hid")
            if first + width < SAMPLES:
                nc.scalar.activation(hid[:], hid_ps[:], RELU, bias=b1_sb[:, 0:1])
            else:
                nc.vector.tensor_scalar(hid[:], hid_ps[:], b1_sb[:, 0:1], 0.0, op0=ADD, op1=MAX)

            if first > 0:
                second_layer(*before, (2, 3))
            out_sb = work.tile([P, VBLOCKS, width], F32, name="out_sb")
            second_layer(first, width, hid, out_sb, (0, 1))
            before = (first, width, hid, out_sb)
            first += width
        second_layer(*before, (2, 3))
